import numpy as np
import ml_dtypes


def mxq(x, axis, fmt="e4m3"):
    dtype, down = {"e4m3": (ml_dtypes.float8_e4m3fn, 7), "e5m2": (ml_dtypes.float8_e5m2, 14)}[fmt]
    v = np.moveaxis(np.asarray(x, np.float32).astype(ml_dtypes.bfloat16).astype(np.float64), axis, -1)
    blocks = v.reshape(v.shape[:-1] + (-1, 32))
    amax = np.abs(blocks).max(-1, keepdims=True)
    byte = np.maximum(np.where(amax > 0, np.frexp(amax)[1] - 1 + 127, 0) - down, 1)
    scale = np.exp2(byte - 127.0)
    codes = (blocks / scale).astype(np.float32).astype(dtype).astype(np.float64)
    return np.moveaxis((codes * scale).reshape(v.shape), -1, axis)


WIDE = False


def mx_kscale(k):
    if not WIDE:
        return np.ones(k)
    levels = np.array([10, -10, 5, -5, 0])
    a = np.random.permutation(np.resize(levels, k // 512 * 4)).reshape(k // 512, 4)
    idx = np.arange(k)
    return np.exp2(a[idx // 512, idx % 128 // 32])


BF16 = ml_dtypes.bfloat16


def bf(x):
    return np.asarray(x, np.float32).astype(BF16)


def f64(x):
    return np.asarray(x).astype(np.float64)


E2M1 = np.array([0.0, 0.5, 1.0, 1.5, 2.0, 3.0, 4.0, 6.0, -0.0, -0.5, -1.0, -1.5, -2.0, -3.0, -4.0, -6.0])


def pack_weight(w, fmt):
    k, n = w.shape
    w = f64(bf(w)).reshape(k // 32, 32, n)
    amax = np.abs(w).max(1)
    if fmt == "e4m3":
        byte = np.frexp(amax)[1] - 1 + 127 - 7
    else:
        mant, ex = np.frexp(amax / 6.0)
        byte = np.where(mant > 0.5, ex, ex - 1) + 127
    byte = np.clip(np.where(amax > 0, byte, 1), 1, 254)
    scaled = (w * np.exp2(127.0 - byte)[:, None, :]).reshape(k, n).astype(np.float32)
    by_word = np.ascontiguousarray(scaled.reshape(k // 512, 128, 4, n).transpose(0, 1, 3, 2))
    if fmt == "e4m3":
        words = by_word.astype(ml_dtypes.float8_e4m3fn).view(np.uint8)
    else:
        c = by_word.astype(ml_dtypes.float4_e2m1fn).view(np.uint8) & 0xF
        words = c[..., 0::2] | (c[..., 1::2] << 4)
    return np.ascontiguousarray(words), np.ascontiguousarray(byte.astype(np.uint8).reshape(k // 512, 16, n))


def unpack_weight(words, scales, fmt):
    g, p, n, _ = words.shape
    if fmt == "e4m3":
        vals = np.ascontiguousarray(words).view(ml_dtypes.float8_e4m3fn).astype(np.float64)
    else:
        nib = np.empty((g, p, n, 4), np.uint8)
        nib[..., 0::2] = words & 0xF
        nib[..., 1::2] = words >> 4
        vals = E2M1[nib]
    vals = vals * np.repeat(np.exp2(scales.astype(np.float64) - 127.0), 8, axis=1)[..., None]
    return vals.transpose(0, 1, 3, 2).reshape(g * 512, n)


B, S, DI, DO = 4, 256, 2048, 2048
R = B * S
LN_EPS = 1e-5
FMT = "e4m3"


def ste_sign(w):
    return np.where(w >= 0, 1.0, -1.0)


def setup_inputs():
    r = np.asarray(mx_kscale(DI), np.float64)[np.arange(R) * DI // R]
    x = bf(np.random.standard_normal((B, S, DI)) * r.reshape(B, S, 1))
    words, scales = pack_weight(ste_sign(np.random.standard_normal((DO, DI)) * 0.02).T, FMT)
    return {"x": x,
            "weight_words": words,
            "weight_scales": scales,
            "in_channel_scale": bf(np.random.uniform(0.5, 1.5, DI) / np.sqrt(DI)),
            "out_channel_scale": bf(np.random.uniform(0.5, 1.5, DO) / r.min()),
            "bias": bf(np.random.standard_normal(DO) * 0.3),
            "ln_gamma": bf(1.0 + 0.1 * np.random.standard_normal(DO)),
            "ln_beta": bf(0.1 * np.random.standard_normal(DO))}


def reference(x, weight_words, weight_scales, in_channel_scale, out_channel_scale, bias, ln_gamma, ln_beta):
    x = f64(x)
    orig_shape = x.shape
    xf = x.reshape(-1, orig_shape[-1])
    w_bin_t = unpack_weight(weight_words, weight_scales, FMT)
    xs = xf * f64(in_channel_scale)
    h = (mxq(xs, 1, "e4m3") @ w_bin_t) * f64(out_channel_scale)
    h = h + f64(bias)
    mu = np.mean(h, axis=-1, keepdims=True)
    var = np.mean(np.square(h - mu), axis=-1, keepdims=True)
    h = (h - mu) / np.sqrt(var + LN_EPS) * f64(ln_gamma) + f64(ln_beta)
    return h.reshape(*orig_shape[:-1], w_bin_t.shape[1])

@@ -1,0 +1,279 @@
+from contextlib import ExitStack
+
+import concourse.masks as masks
+import concourse.mybir as mybir
+
+F32 = mybir.dt.float32
+BF16 = mybir.dt.bfloat16
+I32 = mybir.dt.int32
+U32 = mybir.dt.uint32
+U8 = mybir.dt.uint8
+FP8X4 = mybir.dt.float8_e4m3fn_x4
+ALU = mybir.AluOpType
+ACT = mybir.ActivationFunctionType
+
+P = 128
+PACK = 4
+K_PASS = P * PACK
+ROWS = 1024
+D_IN = 2048
+D_OUT = 2048
+PASSES = D_IN // K_PASS
+ROW_TILES = ROWS // P
+CHANNEL_TILES = D_OUT // P
+BANK = 512
+BANKS_PER_ROW = D_OUT // BANK
+BLOCK_ROWS = 128
+TILES_PER_BLOCK = BLOCK_ROWS // P
+CHANNEL_TILES_PER_BANK = BANK // BLOCK_ROWS
+QUANT_PASSES = min(PASSES, 4096 // (BLOCK_ROWS * PACK))
+HALF = D_OUT // 2
+LN_EPS = 1e-5
+FLOPS = 2 * ROWS * D_IN * D_OUT
+
+
+def valid(row_tile):
+    return 0 <= row_tile < ROW_TILES
+
+
+def tile_onebitlinear_kernel(
+    tc, x, weight_words, weight_scales, in_channel_scale, out_channel_scale, bias, ln_gamma, ln_beta, out
+):
+    nc = tc.nc
+    x_rows = x.flatten_outer_dims()
+    out_rows = out.flatten_outer_dims()
+
+    with ExitStack() as ctx:
+        const = ctx.enter_context(tc.tile_pool(name="const", bufs=1))
+        xin = ctx.enter_context(tc.tile_pool(name="xin", bufs=ROW_TILES))
+        xprep = ctx.enter_context(tc.tile_pool(name="xprep", bufs=2))
+        hpool = ctx.enter_context(tc.tile_pool(name="hpool", bufs=2))
+        work = ctx.enter_context(tc.tile_pool(name="work", bufs=2))
+        small = ctx.enter_context(tc.tile_pool(name="small", bufs=3))
+        psum_mm = ctx.enter_context(tc.psum_pool(name="psum_mm", bufs=2))
+        psum_t = ctx.enter_context(tc.psum_pool(name="psum_t", bufs=6))
+        ctx.enter_context(tc.manual_schedule())
+
+        ident = const.tile([P, P], F32)
+        masks.make_identity(nc, ident[:])
+        eps = const.tile([P, 1], F32)
+        nc.vector.memset(eps[:], LN_EPS)
+
+        s_bc = const.tile([P, D_IN], BF16)
+        nc.scalar.dma_start(out=s_bc[:], in_=in_channel_scale.partition_broadcast(P))
+
+        x_tiles = {}
+
+        def load_x(t):
+            x_tiles[t] = xin.tile([P, D_IN], BF16, name="x_sb")
+            nc.sync.dma_start(out=x_tiles[t][:], in_=x_rows[t * P : (t + 1) * P, :])
+
+        for t in range(TILES_PER_BLOCK):
+            load_x(t)
+
+        vec_rows_bf = const.tile([P, P], BF16)
+        nc.vector.memset(vec_rows_bf[:], 0.0)
+        nc.scalar.dma_start(
+            out=vec_rows_bf[0:CHANNEL_TILES, :], in_=out_channel_scale.rearrange("(j c) -> j c", c=P)
+        )
+        nc.scalar.dma_start(
+            out=vec_rows_bf[CHANNEL_TILES : 2 * CHANNEL_TILES, :], in_=bias.rearrange("(j c) -> j c", c=P)
+        )
+
+        w_planes = const.tile([P, D_OUT], U8, align_bytes=64)
+        nc.vector.memset(w_planes[:].bitcast(I32), 0)
+        for quadrant in range(4):
+            nc.sync.dma_start(
+                out=w_planes[32 * quadrant : 32 * quadrant + 16, :].bitcast(I32),
+                in_=weight_scales[:, 4 * quadrant : 4 * quadrant + 4, :].bitcast(I32),
+            )
+
+        w_words = const.tile([P, PASSES, D_OUT], U32, align_bytes=64)
+        w_bytes = weight_words.rearrange("g p n t -> p g (n t)")
+        for c in range(BANKS_PER_ROW):
+            nc.sync.dma_start(
+                out=w_words[:, :, c * BANK : (c + 1) * BANK].bitcast(I32),
+                in_=w_bytes[:, :, c * BANK * PACK : (c + 1) * BANK * PACK].bitcast(I32),
+            )
+            if valid(TILES_PER_BLOCK + c):
+                load_x(TILES_PER_BLOCK + c)
+        for t in range(TILES_PER_BLOCK + BANKS_PER_ROW, ROW_TILES):
+            load_x(t)
+
+        gamma_bc = const.tile([P, D_OUT], BF16)
+        nc.sync.dma_start(out=gamma_bc[:], in_=ln_gamma.partition_broadcast(P))
+        beta_bc = const.tile([P, D_OUT], BF16)
+        nc.sync.dma_start(out=beta_bc[:], in_=ln_beta.partition_broadcast(P))
+
+        vec_rows = const.tile([P, P], F32)
+        nc.scalar.copy(out=vec_rows[:], in_=vec_rows_bf[:])
+        vec_cols = psum_t.tile([P, BANK], F32, name="vec_cols", tag="t_bank")
+        nc.tensor.transpose(vec_cols[:, 0:P], vec_rows[:], ident[:])
+        scale_bias = const.tile([P, 2 * CHANNEL_TILES], F32)
+        nc.scalar.copy(out=scale_bias[:], in_=vec_cols[:, 0 : 2 * CHANNEL_TILES])
+
+        xs_tiles, xt_banks, grouped, codes, planes = {}, {}, {}, {}, {}
+        h_t, h_banks, h_rows, h_sums, neg_mean, sq_sums, res = {}, {}, {}, {}, {}, {}, {}
+
+        def scale_rows(t):
+            xs_tiles[t] = xprep.tile([P, D_IN], BF16, name="xs")
+            nc.vector.tensor_tensor(out=xs_tiles[t][:], in0=x_tiles[t][:], in1=s_bc[:], op=ALU.mult)
+
+        def transpose_x(t):
+            xs_words = xs_tiles[t][:].bitcast(F32)
+            xt_banks[t] = []
+            for pair in range(PASSES // 2):
+                xt = psum_t.tile([P, 2, 2, P], F32, name="xt", tag="t_bank")
+                for gg in range(2):
+                    g = 2 * pair + gg
+                    for u in range(2):
+                        nc.tensor.transpose(
+                            xt[:, gg, u, :], xs_words[:, 256 * g + u : 256 * (g + 1) : 2], ident[:]
+                        )
+                xt_banks[t].append(xt)
+
+        def regroup_x(t):
+            block, part = divmod(t, TILES_PER_BLOCK)
+            if part == 0:
+                grouped[block] = xprep.tile(
+                    [P, PASSES, BLOCK_ROWS, PACK], BF16, name="grouped", align_bytes=64
+                )
+            grouped_words = grouped[block][:].bitcast(F32)
+            for pair in range(PASSES // 2):
+                nc.vector.tensor_copy(
+                    out=grouped_words[:, 2 * pair : 2 * pair + 2, part * P : (part + 1) * P, :],
+                    in_=xt_banks[t][pair][:].rearrange("p g u r -> p g r u"),
+                )
+            if part == TILES_PER_BLOCK - 1:
+                codes[block] = xprep.tile([P, PASSES, BLOCK_ROWS], U32, name="x_codes", align_bytes=64)
+                planes[block] = xprep.tile([P, PASSES, BLOCK_ROWS], U8, name="x_planes", align_bytes=64)
+                for g0 in range(0, PASSES, QUANT_PASSES):
+                    some = slice(g0, g0 + QUANT_PASSES)
+                    nc.vector.quantize_mx(
+                        out=codes[block][:, some, :].rearrange("p g r -> p (g r)").bitcast(FP8X4),
+                        scales=planes[block][:, some, :].rearrange("p g r -> p (g r)"),
+                        in_=grouped[block][:, some, :, :].rearrange("p g r t -> p (g r t)"),
+                    )
+
+        def linear_bank(step, bank):
+            block, part = divmod(step, TILES_PER_BLOCK)
+            if part == 0 and bank == 0:
+                h_t[block] = hpool.tile([P, CHANNEL_TILES, BLOCK_ROWS], F32, name="h_t")
+            acc = psum_mm.tile([P, CHANNEL_TILES_PER_BANK, BLOCK_ROWS], F32, name="acc")
+            first = (part * BANKS_PER_ROW + bank) * CHANNEL_TILES_PER_BANK
+            for jj in range(CHANNEL_TILES_PER_BANK):
+                chans = slice((first + jj) * P, (first + jj + 1) * P)
+                for g in range(PASSES):
+                    nc.tensor.matmul_mx(
+                        out=acc[:, jj, :],
+                        lhsT=w_words[:, g, chans].bitcast(FP8X4),
+                        lhsT_scale=w_planes[4 * g : P, chans],
+                        rhs=codes[block][:, g, :].bitcast(FP8X4),
+                        rhs_scale=planes[block][:, g, :],
+                        start=(g == 0),
+                        stop=(g == PASSES - 1),
+                    )
+            for jj in range(CHANNEL_TILES_PER_BANK):
+                j = first + jj
+                nc.scalar.activation(
+                    out=h_t[block][:, j, :],
+                    in_=acc[:, jj, :],
+                    func=ACT.Identity,
+                    scale=scale_bias[:, j : j + 1],
+                    bias=scale_bias[:, CHANNEL_TILES + j : CHANNEL_TILES + j + 1],
+                )
+
+        def transpose_h(t):
+            block, part = divmod(t, TILES_PER_BLOCK)
+            h_banks[t] = []
+            for c in range(BANKS_PER_ROW):
+                h_bank = psum_t.tile([P, BANK], F32, name="h_bank", tag="t_bank")
+                for jj in range(BANK // P):
+                    nc.tensor.transpose(
+                        h_bank[:, jj * P : (jj + 1) * P],
+                        h_t[block][:, c * (BANK // P) + jj, part * P : (part + 1) * P],
+                        ident[:],
+                    )
+                h_banks[t].append(h_bank)
+
+        def row_sums(t, c):
+            if c == 0:
+                h_rows[t] = work.tile([P, D_OUT], F32, name="h_rows")
+                h_sums[t] = small.tile([P, BANKS_PER_ROW], F32, name="h_sums")
+            nc.scalar.activation(
+                out=h_rows[t][:, c * BANK : (c + 1) * BANK],
+                in_=h_banks[t][c][:],
+                func=ACT.Copy,
+                accum_out=h_sums[t][:, c : c + 1],
+            )
+
+        def mean(t):
+            scaled_sums = small.tile([P, BANKS_PER_ROW], F32, name="scaled_sums")
+            neg_mean[t] = small.tile([P, 1], F32, name="neg_mean")
+            nc.scalar.activation(
+                out=scaled_sums[:], in_=h_sums[t][:], func=ACT.Copy, scale=-1.0 / D_OUT, accum_out=neg_mean[t][:]
+            )
+
+        def centre_and_gain(t):
+            res[t] = work.tile([P, D_OUT], F32, name="res")
+            nc.vector.scalar_tensor_tensor(
+                out=res[t][:], in0=h_rows[t][:], scalar=neg_mean[t][:], in1=gamma_bc[:], op0=ALU.add, op1=ALU.mult
+            )
+
+        def square_sums(t, half):
+            if half == 0:
+                sq_sums[t] = small.tile([P, 2], F32, name="sq_sums")
+            squares = work.tile([P, HALF], F32, name="squares")
+            nc.scalar.activation(
+                out=squares[:],
+                in_=h_rows[t][:, half * HALF : (half + 1) * HALF],
+                func=ACT.Square,
+                bias=neg_mean[t][:],
+                scale=1.0,
+                accum_out=sq_sums[t][:, half : half + 1],
+            )
+
+        def finish_rows(t):
+            scaled_sq = small.tile([P, 2], F32, name="scaled_sq")
+            var = small.tile([P, 1], F32, name="var")
+            nc.scalar.activation(
+                out=scaled_sq[:], in_=sq_sums[t][:], func=ACT.Copy, scale=1.0 / D_OUT, accum_out=var[:]
+            )
+            std = small.tile([P, 1], F32, name="std")
+            nc.scalar.activation(out=std[:], in_=var[:], func=ACT.Sqrt, bias=eps[:], scale=1.0)
+            rstd = small.tile([P, 1], F32, name="rstd")
+            nc.vector.reciprocal(rstd[:], std[:])
+            for half in range(2):
+                cols = slice(half * HALF, (half + 1) * HALF)
+                nc.vector.scalar_tensor_tensor(
+                    out=res[t][:, cols], in0=res[t][:, cols], scalar=rstd[:], in1=beta_bc[:, cols],
+                    op0=ALU.mult, op1=ALU.add,
+                )
+                nc.sync.dma_start(out=out_rows[t * P : (t + 1) * P, cols], in_=res[t][:, cols])
+
+        for step in range(-(TILES_PER_BLOCK + 1), ROW_TILES + TILES_PER_BLOCK + 1):
+            ahead = step + TILES_PER_BLOCK
+            back = step - TILES_PER_BLOCK
+            last = back - 1
+            if valid(last):
+                centre_and_gain(last)
+            if valid(ahead + 1):
+                scale_rows(ahead + 1)
+            if valid(ahead):
+                regroup_x(ahead)
+            for bank in range(BANKS_PER_ROW):
+                if valid(step):
+                    linear_bank(step, bank)
+                if bank < 2 and valid(last):
+                    square_sums(last, bank)
+                if bank == 1 and valid(last):
+                    finish_rows(last)
+                if bank == 1 and valid(back):
+                    transpose_h(back)
+                if bank >= 2 and valid(back):
+                    row_sums(back, 2 * bank - 4)
+                    row_sums(back, 2 * bank - 3)
+            if valid(back):
+                mean(back)
+            if valid(ahead + 1):
+                transpose_x(ahead + 1)

@@ -23,7 +23,7 @@ ROW_TILES = ROWS // P
 CHANNEL_TILES = D_OUT // P
 BANK = 512
 BANKS_PER_ROW = D_OUT // BANK
-BLOCK_ROWS = 128
+BLOCK_ROWS = 256
 TILES_PER_BLOCK = BLOCK_ROWS // P
 CHANNEL_TILES_PER_BANK = BANK // BLOCK_ROWS
 QUANT_PASSES = min(PASSES, 4096 // (BLOCK_ROWS * PACK))

@@ -23,7 +23,7 @@ ROW_TILES = ROWS // P
 CHANNEL_TILES = D_OUT // P
 BANK = 512
 BANKS_PER_ROW = D_OUT // BANK
-BLOCK_ROWS = 256
+BLOCK_ROWS = 128
 TILES_PER_BLOCK = BLOCK_ROWS // P
 CHANNEL_TILES_PER_BANK = BANK // BLOCK_ROWS
 QUANT_PASSES = min(PASSES, 4096 // (BLOCK_ROWS * PACK))
@@ -59,8 +59,9 @@ def tile_onebitlinear_kernel(
         eps = const.tile([P, 1], F32)
         nc.vector.memset(eps[:], LN_EPS)
 
-        s_bc = const.tile([P, D_IN], BF16)
-        nc.scalar.dma_start(out=s_bc[:], in_=in_channel_scale.partition_broadcast(P))
+        s_rows = const.tile([P, D_IN], BF16)
+        nc.vector.memset(s_rows[:].bitcast(I32), 0)
+        nc.scalar.dma_start(out=s_rows[0:1, :], in_=in_channel_scale.rearrange("(o k) -> o k", o=1))
 
         x_tiles = {}
 
@@ -95,15 +96,19 @@ def tile_onebitlinear_kernel(
                 out=w_words[:, :, c * BANK : (c + 1) * BANK].bitcast(I32),
                 in_=w_bytes[:, :, c * BANK * PACK : (c + 1) * BANK * PACK].bitcast(I32),
             )
-            if valid(TILES_PER_BLOCK + c):
-                load_x(TILES_PER_BLOCK + c)
-        for t in range(TILES_PER_BLOCK + BANKS_PER_ROW, ROW_TILES):
+            if c == 1:
+                for t in range(TILES_PER_BLOCK, 2 * TILES_PER_BLOCK):
+                    load_x(t)
+        for t in range(2 * TILES_PER_BLOCK, ROW_TILES):
             load_x(t)
 
         gamma_bc = const.tile([P, D_OUT], BF16)
         nc.sync.dma_start(out=gamma_bc[:], in_=ln_gamma.partition_broadcast(P))
         beta_bc = const.tile([P, D_OUT], BF16)
         nc.sync.dma_start(out=beta_bc[:], in_=ln_beta.partition_broadcast(P))
+
+        first_table = const.tile([P, 1], F32)
+        nc.scalar.activation(out=first_table[:], in_=eps[:], func=ACT.Sqrt)
 
         vec_rows = const.tile([P, P], F32)
         nc.scalar.copy(out=vec_rows[:], in_=vec_rows_bf[:])
@@ -112,37 +117,41 @@ def tile_onebitlinear_kernel(
         scale_bias = const.tile([P, 2 * CHANNEL_TILES], F32)
         nc.scalar.copy(out=scale_bias[:], in_=vec_cols[:, 0 : 2 * CHANNEL_TILES])
 
-        xs_tiles, xt_banks, grouped, codes, planes = {}, {}, {}, {}, {}
+        xt_banks, grouped, codes, planes = {}, {}, {}, {}
         h_t, h_banks, h_rows, h_sums, neg_mean, sq_sums, res = {}, {}, {}, {}, {}, {}, {}
 
-        def scale_rows(t):
-            xs_tiles[t] = xprep.tile([P, D_IN], BF16, name="xs")
-            nc.vector.tensor_tensor(out=xs_tiles[t][:], in0=x_tiles[t][:], in1=s_bc[:], op=ALU.mult)
-
-        def transpose_x(t):
-            xs_words = xs_tiles[t][:].bitcast(F32)
-            xt_banks[t] = []
+        def transpose_words(rows_bf16):
+            words = rows_bf16[:].bitcast(F32)
+            banks = []
             for pair in range(PASSES // 2):
                 xt = psum_t.tile([P, 2, 2, P], F32, name="xt", tag="t_bank")
                 for gg in range(2):
                     g = 2 * pair + gg
                     for u in range(2):
-                        nc.tensor.transpose(
-                            xt[:, gg, u, :], xs_words[:, 256 * g + u : 256 * (g + 1) : 2], ident[:]
-                        )
-                xt_banks[t].append(xt)
+                        nc.tensor.transpose(xt[:, gg, u, :], words[:, 256 * g + u : 256 * (g + 1) : 2], ident[:])
+                banks.append(xt)
+            return banks
 
-        def regroup_x(t):
+        s_cols = const.tile([P, PASSES, PACK], BF16)
+        s_banks = transpose_words(s_rows)
+        for pair in range(PASSES // 2):
+            nc.vector.tensor_copy(
+                out=s_cols[:].bitcast(F32)[:, 2 * pair : 2 * pair + 2, :], in_=s_banks[pair][:, :, :, 0]
+            )
+
+        def scale_and_quantise(t):
             block, part = divmod(t, TILES_PER_BLOCK)
             if part == 0:
                 grouped[block] = xprep.tile(
                     [P, PASSES, BLOCK_ROWS, PACK], BF16, name="grouped", align_bytes=64
                 )
-            grouped_words = grouped[block][:].bitcast(F32)
-            for pair in range(PASSES // 2):
-                nc.vector.tensor_copy(
-                    out=grouped_words[:, 2 * pair : 2 * pair + 2, part * P : (part + 1) * P, :],
-                    in_=xt_banks[t][pair][:].rearrange("p g u r -> p g r u"),
+            for g in range(PASSES):
+                x_t = xt_banks[t][g // 2][:].bitcast(BF16).rearrange("p g u (r e) -> p g r u e", e=2)
+                nc.vector.tensor_tensor(
+                    out=grouped[block][:, g, part * P : (part + 1) * P, :].rearrange("p r (u e) -> p r u e", e=2),
+                    in0=x_t[:, g % 2],
+                    in1=s_cols[:, g, :].rearrange("p (u e) -> p u e", e=2).unsqueeze(1).to_broadcast([P, P, 2, 2]),
+                    op=ALU.mult,
                 )
             if part == TILES_PER_BLOCK - 1:
                 codes[block] = xprep.tile([P, PASSES, BLOCK_ROWS], U32, name="x_codes", align_bytes=64)
@@ -255,12 +264,10 @@ def tile_onebitlinear_kernel(
             ahead = step + TILES_PER_BLOCK
             back = step - TILES_PER_BLOCK
             last = back - 1
+            if valid(ahead):
+                scale_and_quantise(ahead)
             if valid(last):
                 centre_and_gain(last)
-            if valid(ahead + 1):
-                scale_rows(ahead + 1)
-            if valid(ahead):
-                regroup_x(ahead)
             for bank in range(BANKS_PER_ROW):
                 if valid(step):
                     linear_bank(step, bank)
@@ -270,10 +277,10 @@ def tile_onebitlinear_kernel(
                     finish_rows(last)
                 if bank == 1 and valid(back):
                     transpose_h(back)
+                if bank == 1 and valid(ahead + 1):
+                    xt_banks[ahead + 1] = transpose_words(x_tiles[ahead + 1])
                 if bank >= 2 and valid(back):
                     row_sums(back, 2 * bank - 4)
                     row_sums(back, 2 * bank - 3)
             if valid(back):
                 mean(back)
-            if valid(ahead + 1):
-                transpose_x(ahead + 1)

@@ -14,26 +14,29 @@ ACT = mybir.ActivationFunctionType
 
 P = 128
 PACK = 4
-K_PASS = P * PACK
 ROWS = 1024
 D_IN = 2048
 D_OUT = 2048
-PASSES = D_IN // K_PASS
+PASSES = D_IN // (P * PACK)
 ROW_TILES = ROWS // P
 CHANNEL_TILES = D_OUT // P
 BANK = 512
 BANKS_PER_ROW = D_OUT // BANK
-BLOCK_ROWS = 128
-TILES_PER_BLOCK = BLOCK_ROWS // P
-CHANNEL_TILES_PER_BANK = BANK // BLOCK_ROWS
-QUANT_PASSES = min(PASSES, 4096 // (BLOCK_ROWS * PACK))
-HALF = D_OUT // 2
 LN_EPS = 1e-5
 FLOPS = 2 * ROWS * D_IN * D_OUT
 
-
-def valid(row_tile):
-    return 0 <= row_tile < ROW_TILES
+SLOTS = [(0, 0), (1, 0), (0, 1), (0, 2), (0, 3), (1, 1), (1, 2), (1, 3)] + [(t, c) for t in range(2, 8) for c in range(4)]
+XLEAD = 4
+XT_AT = {t: SLOTS.index((t, 0)) - XLEAD for t in range(2, 8)}
+HT_AT = {t: SLOTS.index((t, 3)) + min(t, 1) for t in range(7)}
+PERM_FROM = 2
+PERM_LEAD = 2
+TAIL = 0
+BLOCKS = tuple((t,) for t in range(ROW_TILES))
+LOADS = ("x0", "p", "x1", "w0", "w1", "w2", "w3", "w4", "w5", "w6", "w7", "x2", "x3", "gb", "x4", "x5", "x6", "x7")
+W_CHUNK = 256
+STD_LAG = 2
+OUT_LAG = 3
 
 
 def tile_onebitlinear_kernel(
@@ -47,33 +50,26 @@ def tile_onebitlinear_kernel(
         const = ctx.enter_context(tc.tile_pool(name="const", bufs=1))
         xin = ctx.enter_context(tc.tile_pool(name="xin", bufs=ROW_TILES))
         xprep = ctx.enter_context(tc.tile_pool(name="xprep", bufs=2))
-        hpool = ctx.enter_context(tc.tile_pool(name="hpool", bufs=2))
-        work = ctx.enter_context(tc.tile_pool(name="work", bufs=2))
+        xperm = ctx.enter_context(tc.tile_pool(name="xperm", bufs=2))
+        hpool = ctx.enter_context(tc.tile_pool(name="hpool", bufs=3))
+        work = ctx.enter_context(tc.tile_pool(name="work", bufs=3))
         small = ctx.enter_context(tc.tile_pool(name="small", bufs=3))
         psum_mm = ctx.enter_context(tc.psum_pool(name="psum_mm", bufs=2))
-        psum_t = ctx.enter_context(tc.psum_pool(name="psum_t", bufs=6))
+        psum_x = ctx.enter_context(tc.psum_pool(name="psum_x", bufs=2))
+        psum_h = ctx.enter_context(tc.psum_pool(name="psum_h", bufs=4))
         ctx.enter_context(tc.manual_schedule())
 
-        ident = const.tile([P, P], F32)
-        masks.make_identity(nc, ident[:])
-        eps = const.tile([P, 1], F32)
-        nc.vector.memset(eps[:], LN_EPS)
-
-        s_rows = const.tile([P, D_IN], BF16)
-        nc.vector.memset(s_rows[:].bitcast(I32), 0)
-        nc.scalar.dma_start(out=s_rows[0:1, :], in_=in_channel_scale.rearrange("(o k) -> o k", o=1))
-
-        x_tiles = {}
-
-        def load_x(t):
-            x_tiles[t] = xin.tile([P, D_IN], BF16, name="x_sb")
-            nc.sync.dma_start(out=x_tiles[t][:], in_=x_rows[t * P : (t + 1) * P, :])
-
-        for t in range(TILES_PER_BLOCK):
-            load_x(t)
-
-        vec_rows_bf = const.tile([P, P], BF16)
+        w_planes = const.tile([P, D_OUT], U8, name="w_planes", align_bytes=64)
+        nc.vector.memset(w_planes[:].bitcast(I32), 0)
+        vec_rows_bf = const.tile([P, P], BF16, name="vec_rows_bf")
         nc.vector.memset(vec_rows_bf[:], 0.0)
+        eps = const.tile([P, 1], F32, name="eps")
+        nc.vector.memset(eps[:], LN_EPS)
+        ident = const.tile([P, P], F32, name="ident")
+        masks.make_identity(nc, ident[:])
+
+        s_cols = const.tile([P, PASSES, PACK], BF16, name="s_cols")
+        nc.scalar.dma_start(out=s_cols[:], in_=in_channel_scale.rearrange("(g p t) -> p g t", p=P, t=PACK))
         nc.scalar.dma_start(
             out=vec_rows_bf[0:CHANNEL_TILES, :], in_=out_channel_scale.rearrange("(j c) -> j c", c=P)
         )
@@ -81,206 +77,251 @@ def tile_onebitlinear_kernel(
             out=vec_rows_bf[CHANNEL_TILES : 2 * CHANNEL_TILES, :], in_=bias.rearrange("(j c) -> j c", c=P)
         )
 
-        w_planes = const.tile([P, D_OUT], U8, align_bytes=64)
-        nc.vector.memset(w_planes[:].bitcast(I32), 0)
-        for quadrant in range(4):
-            nc.sync.dma_start(
-                out=w_planes[32 * quadrant : 32 * quadrant + 16, :].bitcast(I32),
-                in_=weight_scales[:, 4 * quadrant : 4 * quadrant + 4, :].bitcast(I32),
-            )
-
-        w_words = const.tile([P, PASSES, D_OUT], U32, align_bytes=64)
+        x_tiles = {}
+        w_words = const.tile([P, PASSES, D_OUT], U32, name="w_words", align_bytes=64)
         w_bytes = weight_words.rearrange("g p n t -> p g (n t)")
-        for c in range(BANKS_PER_ROW):
-            nc.sync.dma_start(
-                out=w_words[:, :, c * BANK : (c + 1) * BANK].bitcast(I32),
-                in_=w_bytes[:, :, c * BANK * PACK : (c + 1) * BANK * PACK].bitcast(I32),
-            )
-            if c == 1:
-                for t in range(TILES_PER_BLOCK, 2 * TILES_PER_BLOCK):
-                    load_x(t)
-        for t in range(2 * TILES_PER_BLOCK, ROW_TILES):
-            load_x(t)
+        gamma_bc = const.tile([P, D_OUT], BF16, name="gamma_bc")
+        beta_bc = const.tile([P, D_OUT], BF16, name="beta_bc")
+        for what in LOADS:
+            if what[0] == "x":
+                t = int(what[1:])
+                x_tiles[t] = xin.tile([P, D_IN], BF16, name="x_sb")
+                halves = 2 if t == 0 else 1
+                for i in range(halves):
+                    cols = slice(i * D_IN // halves, (i + 1) * D_IN // halves)
+                    nc.sync.dma_start(out=x_tiles[t][:, cols], in_=x_rows[t * P : (t + 1) * P, cols])
+            elif what == "p":
+                for q in range(4):
+                    nc.scalar.dma_start(
+                        out=w_planes[32 * q : 32 * q + 16, :].bitcast(I32),
+                        in_=weight_scales[:, 4 * q : 4 * q + 4, :].bitcast(I32),
+                    )
+            elif what[0] == "w":
+                c = int(what[1:])
+                nc.sync.dma_start(
+                    out=w_words[:, :, c * W_CHUNK : (c + 1) * W_CHUNK].bitcast(I32),
+                    in_=w_bytes[:, :, c * W_CHUNK * PACK : (c + 1) * W_CHUNK * PACK].bitcast(I32),
+                )
+            else:
+                nc.sync.dma_start(out=gamma_bc[:], in_=ln_gamma.partition_broadcast(P))
+                nc.sync.dma_start(out=beta_bc[:], in_=ln_beta.partition_broadcast(P))
 
-        gamma_bc = const.tile([P, D_OUT], BF16)
-        nc.sync.dma_start(out=gamma_bc[:], in_=ln_gamma.partition_broadcast(P))
-        beta_bc = const.tile([P, D_OUT], BF16)
-        nc.sync.dma_start(out=beta_bc[:], in_=ln_beta.partition_broadcast(P))
-
-        first_table = const.tile([P, 1], F32)
+        first_table = const.tile([P, 1], F32, name="first_table")
         nc.scalar.activation(out=first_table[:], in_=eps[:], func=ACT.Sqrt)
+        vec_rows = const.tile([P, P], F32, name="vec_rows")
+        scale_bias = const.tile([P, 2 * CHANNEL_TILES], F32, name="scale_bias")
 
-        vec_rows = const.tile([P, P], F32)
-        nc.scalar.copy(out=vec_rows[:], in_=vec_rows_bf[:])
-        vec_cols = psum_t.tile([P, BANK], F32, name="vec_cols", tag="t_bank")
-        nc.tensor.transpose(vec_cols[:, 0:P], vec_rows[:], ident[:])
-        scale_bias = const.tile([P, 2 * CHANNEL_TILES], F32)
-        nc.scalar.copy(out=scale_bias[:], in_=vec_cols[:, 0 : 2 * CHANNEL_TILES])
+        perm = {}
+        xt, grouped, codes, planes = {}, {}, {}, {}
+        h_t, h_banks, stats, mv, rstd, res, fin = {}, {}, {}, {}, {}, {}, {}
+        block_of = {t: b for b, tiles in enumerate(BLOCKS) for t in tiles}
 
-        xt_banks, grouped, codes, planes = {}, {}, {}, {}
-        h_t, h_banks, h_rows, h_sums, neg_mean, sq_sums, res = {}, {}, {}, {}, {}, {}, {}
+        def permute_x(t):
+            perm[t] = xperm.tile([P, PASSES, 2, P], F32, name="x_perm", align_bytes=64)
+            nc.scalar.copy(
+                out=perm[t][:], in_=x_tiles[t][:].bitcast(F32).rearrange("p (g w u) -> p g u w", g=PASSES, u=2)
+            )
 
-        def transpose_words(rows_bf16):
-            words = rows_bf16[:].bitcast(F32)
-            banks = []
+        def transpose_x(t):
+            words = x_tiles[t][:].bitcast(F32)
+            xt[t] = []
             for pair in range(PASSES // 2):
-                xt = psum_t.tile([P, 2, 2, P], F32, name="xt", tag="t_bank")
+                bank = psum_x.tile([P, 2, 2, P], F32, name="xt", tag="xt")
                 for gg in range(2):
                     g = 2 * pair + gg
                     for u in range(2):
-                        nc.tensor.transpose(xt[:, gg, u, :], words[:, 256 * g + u : 256 * (g + 1) : 2], ident[:])
-                banks.append(xt)
-            return banks
+                        if t in perm:
+                            some = perm[t][:, g, u, :]
+                        else:
+                            some = words[:, 256 * g + u : 256 * (g + 1) : 2]
+                        nc.tensor.transpose(bank[:, gg, u, :], some, ident[:])
+                xt[t].append(bank)
 
-        s_cols = const.tile([P, PASSES, PACK], BF16)
-        s_banks = transpose_words(s_rows)
-        for pair in range(PASSES // 2):
-            nc.vector.tensor_copy(
-                out=s_cols[:].bitcast(F32)[:, 2 * pair : 2 * pair + 2, :], in_=s_banks[pair][:, :, :, 0]
-            )
-
-        def scale_and_quantise(t):
-            block, part = divmod(t, TILES_PER_BLOCK)
+        def scale_x(t):
+            b = block_of[t]
+            n = P * len(BLOCKS[b])
+            part = BLOCKS[b].index(t)
             if part == 0:
-                grouped[block] = xprep.tile(
-                    [P, PASSES, BLOCK_ROWS, PACK], BF16, name="grouped", align_bytes=64
-                )
+                grouped[b] = xprep.tile([P, PASSES, n, PACK], BF16, name="grouped", align_bytes=64)
             for g in range(PASSES):
-                x_t = xt_banks[t][g // 2][:].bitcast(BF16).rearrange("p g u (r e) -> p g r u e", e=2)
+                x_t = xt[t][g // 2][:].bitcast(BF16).rearrange("p g u (r e) -> p g r u e", e=2)
                 nc.vector.tensor_tensor(
-                    out=grouped[block][:, g, part * P : (part + 1) * P, :].rearrange("p r (u e) -> p r u e", e=2),
+                    out=grouped[b][:, g, part * P : (part + 1) * P, :].rearrange("p r (u e) -> p r u e", e=2),
                     in0=x_t[:, g % 2],
                     in1=s_cols[:, g, :].rearrange("p (u e) -> p u e", e=2).unsqueeze(1).to_broadcast([P, P, 2, 2]),
                     op=ALU.mult,
                 )
-            if part == TILES_PER_BLOCK - 1:
-                codes[block] = xprep.tile([P, PASSES, BLOCK_ROWS], U32, name="x_codes", align_bytes=64)
-                planes[block] = xprep.tile([P, PASSES, BLOCK_ROWS], U8, name="x_planes", align_bytes=64)
-                for g0 in range(0, PASSES, QUANT_PASSES):
-                    some = slice(g0, g0 + QUANT_PASSES)
-                    nc.vector.quantize_mx(
-                        out=codes[block][:, some, :].rearrange("p g r -> p (g r)").bitcast(FP8X4),
-                        scales=planes[block][:, some, :].rearrange("p g r -> p (g r)"),
-                        in_=grouped[block][:, some, :, :].rearrange("p g r t -> p (g r t)"),
-                    )
 
-        def linear_bank(step, bank):
-            block, part = divmod(step, TILES_PER_BLOCK)
-            if part == 0 and bank == 0:
-                h_t[block] = hpool.tile([P, CHANNEL_TILES, BLOCK_ROWS], F32, name="h_t")
-            acc = psum_mm.tile([P, CHANNEL_TILES_PER_BANK, BLOCK_ROWS], F32, name="acc")
-            first = (part * BANKS_PER_ROW + bank) * CHANNEL_TILES_PER_BANK
-            for jj in range(CHANNEL_TILES_PER_BANK):
-                chans = slice((first + jj) * P, (first + jj + 1) * P)
+        def quantise(b):
+            n = P * len(BLOCKS[b])
+            codes[b] = xprep.tile([P, PASSES, n], U32, name="x_codes", align_bytes=64)
+            planes[b] = xprep.tile([P, PASSES, n], U8, name="x_planes", align_bytes=64)
+            step = min(PASSES, 2048 // (n * PACK))
+            for g0 in range(0, PASSES, step):
+                some = slice(g0, g0 + step)
+                nc.vector.quantize_mx(
+                    out=codes[b][:, some, :].rearrange("p g r -> p (g r)").bitcast(FP8X4),
+                    scales=planes[b][:, some, :].rearrange("p g r -> p (g r)"),
+                    in_=grouped[b][:, some, :, :].rearrange("p g r t -> p (g r t)"),
+                )
+
+        def linear(b, bank):
+            n = P * len(BLOCKS[b])
+            per = BANK // n
+            if bank == 0:
+                h_t[b] = hpool.tile([P, CHANNEL_TILES, n], F32, name="h_t")
+            acc = psum_mm.tile([P, per, n], F32, name="acc")
+            for jj in range(per):
+                chans = slice((bank * per + jj) * P, (bank * per + jj + 1) * P)
                 for g in range(PASSES):
                     nc.tensor.matmul_mx(
                         out=acc[:, jj, :],
                         lhsT=w_words[:, g, chans].bitcast(FP8X4),
                         lhsT_scale=w_planes[4 * g : P, chans],
-                        rhs=codes[block][:, g, :].bitcast(FP8X4),
-                        rhs_scale=planes[block][:, g, :],
+                        rhs=codes[b][:, g, :].bitcast(FP8X4),
+                        rhs_scale=planes[b][:, g, :],
                         start=(g == 0),
                         stop=(g == PASSES - 1),
                     )
-            for jj in range(CHANNEL_TILES_PER_BANK):
-                j = first + jj
+            for jj in range(per):
+                j = bank * per + jj
                 nc.scalar.activation(
-                    out=h_t[block][:, j, :],
+                    out=h_t[b][:, j, :],
                     in_=acc[:, jj, :],
                     func=ACT.Identity,
                     scale=scale_bias[:, j : j + 1],
                     bias=scale_bias[:, CHANNEL_TILES + j : CHANNEL_TILES + j + 1],
                 )
 
-        def transpose_h(t):
-            block, part = divmod(t, TILES_PER_BLOCK)
-            h_banks[t] = []
-            for c in range(BANKS_PER_ROW):
-                h_bank = psum_t.tile([P, BANK], F32, name="h_bank", tag="t_bank")
-                for jj in range(BANK // P):
-                    nc.tensor.transpose(
-                        h_bank[:, jj * P : (jj + 1) * P],
-                        h_t[block][:, c * (BANK // P) + jj, part * P : (part + 1) * P],
-                        ident[:],
-                    )
-                h_banks[t].append(h_bank)
-
-        def row_sums(t, c):
+        def transpose_h(t, c):
+            b = block_of[t]
+            part = BLOCKS[b].index(t)
             if c == 0:
-                h_rows[t] = work.tile([P, D_OUT], F32, name="h_rows")
-                h_sums[t] = small.tile([P, BANKS_PER_ROW], F32, name="h_sums")
-            nc.scalar.activation(
-                out=h_rows[t][:, c * BANK : (c + 1) * BANK],
-                in_=h_banks[t][c][:],
-                func=ACT.Copy,
-                accum_out=h_sums[t][:, c : c + 1],
-            )
-
-        def mean(t):
-            scaled_sums = small.tile([P, BANKS_PER_ROW], F32, name="scaled_sums")
-            neg_mean[t] = small.tile([P, 1], F32, name="neg_mean")
-            nc.scalar.activation(
-                out=scaled_sums[:], in_=h_sums[t][:], func=ACT.Copy, scale=-1.0 / D_OUT, accum_out=neg_mean[t][:]
-            )
-
-        def centre_and_gain(t):
-            res[t] = work.tile([P, D_OUT], F32, name="res")
-            nc.vector.scalar_tensor_tensor(
-                out=res[t][:], in0=h_rows[t][:], scalar=neg_mean[t][:], in1=gamma_bc[:], op0=ALU.add, op1=ALU.mult
-            )
-
-        def square_sums(t, half):
-            if half == 0:
-                sq_sums[t] = small.tile([P, 2], F32, name="sq_sums")
-            squares = work.tile([P, HALF], F32, name="squares")
-            nc.scalar.activation(
-                out=squares[:],
-                in_=h_rows[t][:, half * HALF : (half + 1) * HALF],
-                func=ACT.Square,
-                bias=neg_mean[t][:],
-                scale=1.0,
-                accum_out=sq_sums[t][:, half : half + 1],
-            )
-
-        def finish_rows(t):
-            scaled_sq = small.tile([P, 2], F32, name="scaled_sq")
-            var = small.tile([P, 1], F32, name="var")
-            nc.scalar.activation(
-                out=scaled_sq[:], in_=sq_sums[t][:], func=ACT.Copy, scale=1.0 / D_OUT, accum_out=var[:]
-            )
-            std = small.tile([P, 1], F32, name="std")
-            nc.scalar.activation(out=std[:], in_=var[:], func=ACT.Sqrt, bias=eps[:], scale=1.0)
-            rstd = small.tile([P, 1], F32, name="rstd")
-            nc.vector.reciprocal(rstd[:], std[:])
-            for half in range(2):
-                cols = slice(half * HALF, (half + 1) * HALF)
-                nc.vector.scalar_tensor_tensor(
-                    out=res[t][:, cols], in0=res[t][:, cols], scalar=rstd[:], in1=beta_bc[:, cols],
-                    op0=ALU.mult, op1=ALU.add,
+                h_banks[t] = []
+            if TAIL and t == ROW_TILES - 1 and c < 2:
+                bank = psum_x.tile([P, BANK], F32, name="h_last", tag="xt")
+            else:
+                bank = psum_h.tile([P, BANK], F32, name="h_bank")
+            for jj in range(4):
+                nc.tensor.transpose(
+                    bank[:, jj * P : (jj + 1) * P], h_t[b][:, 4 * c + jj, part * P : (part + 1) * P], ident[:]
                 )
-                nc.sync.dma_start(out=out_rows[t * P : (t + 1) * P, cols], in_=res[t][:, cols])
+            h_banks[t].append(bank)
 
-        for step in range(-(TILES_PER_BLOCK + 1), ROW_TILES + TILES_PER_BLOCK + 1):
-            ahead = step + TILES_PER_BLOCK
-            back = step - TILES_PER_BLOCK
-            last = back - 1
-            if valid(ahead):
-                scale_and_quantise(ahead)
-            if valid(last):
-                centre_and_gain(last)
-            for bank in range(BANKS_PER_ROW):
-                if valid(step):
-                    linear_bank(step, bank)
-                if bank < 2 and valid(last):
-                    square_sums(last, bank)
-                if bank == 1 and valid(last):
-                    finish_rows(last)
-                if bank == 1 and valid(back):
-                    transpose_h(back)
-                if bank == 1 and valid(ahead + 1):
-                    xt_banks[ahead + 1] = transpose_words(x_tiles[ahead + 1])
-                if bank >= 2 and valid(back):
-                    row_sums(back, 2 * bank - 4)
-                    row_sums(back, 2 * bank - 3)
-            if valid(back):
-                mean(back)
+        def row_stats(t, c):
+            if c == 0:
+                stats[t] = small.tile([P, BANKS_PER_ROW, 6], F32, name="stats")
+            nc.vector.bn_stats(out=stats[t][:, c, :], in_=h_banks[t][c][:])
+
+        def aggregate(t):
+            mv[t] = small.tile([P, 2], F32, name="mean_var")
+            nc.vector.bn_aggr(out=mv[t][:], in_=stats[t][:].rearrange("p c s -> p (c s)"))
+
+        def centre_and_gain(t, c):
+            if c == 0:
+                res[t] = work.tile([P, D_OUT], F32, name="res")
+            cols = slice(c * BANK, (c + 1) * BANK)
+            nc.vector.scalar_tensor_tensor(
+                out=res[t][:, cols], in0=h_banks[t][c][:], scalar=mv[t][:, 0:1], in1=gamma_bc[:, cols],
+                op0=ALU.subtract, op1=ALU.mult,
+            )
+
+        def std_dev(t):
+            rstd[t] = small.tile([P, 2], F32, name="rstd")
+            nc.scalar.activation(out=rstd[t][:, 0:1], in_=mv[t][:, 1:2], func=ACT.Sqrt, bias=eps[:], scale=1.0)
+
+        def inverse_std(t):
+            nc.vector.reciprocal(rstd[t][:, 1:2], rstd[t][:, 0:1])
+
+        def scale_rows(t, c):
+            if c == 0:
+                fin[t] = work.tile([P, D_OUT], F32, name="fin")
+            cols = slice(c * BANK, (c + 1) * BANK)
+            nc.scalar.activation(out=fin[t][:, cols], in_=res[t][:, cols], func=ACT.Copy, scale=rstd[t][:, 1:2])
+            nc.gpsimd.tensor_tensor(out=fin[t][:, cols], in0=fin[t][:, cols], in1=beta_bc[:, cols], op=ALU.add)
+            if c % 2:
+                store(t, fin[t], c - 1, c + 1)
+
+        def store(t, tile, c0, c1):
+            cols = slice(c0 * BANK, c1 * BANK)
+            nc.sync.dma_start(out=out_rows[t * P : (t + 1) * P, cols], in_=tile[:, cols])
+
+        def finish_on_vector(t, c):
+            cols = slice(c * BANK, (c + 1) * BANK)
+            nc.vector.scalar_tensor_tensor(
+                out=res[t][:, cols], in0=res[t][:, cols], scalar=rstd[t][:, 1:2], in1=beta_bc[:, cols],
+                op0=ALU.mult, op1=ALU.add,
+            )
+            store(t, res[t], c, c + 1)
+
+        later = {}
+        transpose_x(0)
+        nc.scalar.copy(out=vec_rows[:], in_=vec_rows_bf[:])
+        scale_x(0)
+        quantise(0)
+        transpose_x(1)
+        scale_x(1)
+        quantise(1)
+        vec_cols = psum_h.tile([P, BANK], F32, name="h_bank")
+        nc.tensor.transpose(vec_cols[:, 0:P], vec_rows[:], ident[:])
+        nc.scalar.copy(out=scale_bias[:], in_=vec_cols[:, 0 : 2 * CHANNEL_TILES])
+        for k, (b, bank) in enumerate(SLOTS):
+            linear(b, bank)
+            for t in range(PERM_FROM, ROW_TILES):
+                if XT_AT[t] - PERM_LEAD == k:
+                    permute_x(t)
+            for job in later.pop(k, []):
+                job()
+            if TAIL:
+                t = ROW_TILES - 1
+                for c in range(2):
+                    if k == SLOTS.index((t, c)) + 1:
+                        transpose_h(t, c)
+                        row_stats(t, c)
+            for t in range(ROW_TILES):
+                if XT_AT.get(t) == k:
+                    transpose_x(t)
+            for t in range(ROW_TILES - 1):
+                if HT_AT.get(t) == k:
+                    for c in range(4):
+                        transpose_h(t, c)
+            for t in range(ROW_TILES):
+                if XT_AT.get(t) == k:
+                    scale_x(t)
+            for t in range(ROW_TILES - 1):
+                if HT_AT.get(t) == k:
+                    for c in range(4):
+                        row_stats(t, c)
+            for t in range(ROW_TILES):
+                if XT_AT.get(t) == k:
+                    quantise(t)
+            for t in range(ROW_TILES - 1):
+                if HT_AT.get(t) == k:
+                    aggregate(t)
+                    for c in range(4):
+                        centre_and_gain(t, c)
+                    later.setdefault(k + STD_LAG, []).append(lambda t=t: (std_dev(t), inverse_std(t)))
+                    for c in range(4):
+                        later.setdefault(k + OUT_LAG + c, []).append(lambda t=t, c=c: scale_rows(t, c))
+        for k in sorted(later):
+            for job in later[k]:
+                job()
+        t = ROW_TILES - 1
+        if not TAIL:
+            for c in range(4):
+                transpose_h(t, c)
+            for c in range(4):
+                row_stats(t, c)
+        else:
+            for c in range(2, 4):
+                transpose_h(t, c)
+                row_stats(t, c)
+        aggregate(t)
+        std_dev(t)
+        centre_and_gain(t, 0)
+        centre_and_gain(t, 1)
+        inverse_std(t)
+        for c in range(4):
+            finish_on_vector(t, c)
+            if c < 2:
+                centre_and_gain(t, c + 2)

@@ -25,18 +25,21 @@ BANKS_PER_ROW = D_OUT // BANK
 LN_EPS = 1e-5
 FLOPS = 2 * ROWS * D_IN * D_OUT
 
-SLOTS = [(0, 0), (1, 0), (0, 1), (0, 2), (0, 3), (1, 1), (1, 2), (1, 3)] + [(t, c) for t in range(2, 8) for c in range(4)]
-XLEAD = 4
-XT_AT = {t: SLOTS.index((t, 0)) - XLEAD for t in range(2, 8)}
-HT_AT = {t: SLOTS.index((t, 3)) + min(t, 1) for t in range(7)}
-PERM_FROM = 2
-PERM_LEAD = 2
-TAIL = 0
 BLOCKS = tuple((t,) for t in range(ROW_TILES))
-LOADS = ("x0", "p", "x1", "w0", "w1", "w2", "w3", "w4", "w5", "w6", "w7", "x2", "x3", "gb", "x4", "x5", "x6", "x7")
+SLOTS = [(0, 0), (1, 0), (0, 1), (1, 1), (0, 2), (0, 3), (1, 2), (1, 3)] + [(t, c) for t in range(2, 8) for c in range(4)]
+HT_AT = {t: SLOTS.index((t, 3)) + min(t, 1) for t in range(7)}
+XT_AT = {t: SLOTS.index((t - 1, 0) if t > 2 else (0, 2)) for t in range(2, 8)}
+PERM_FROM = 3
+PERM_LEAD = 2
+S_STATS = {}
+G_GAIN = {}
+LOADS = ('x0', 'p', 'x1', 'w0', 'w1', 'w2', 'w3', 'w4', 'w5', 'x2', 'w6', 'w7', 'x3', 'gb', 'x4', 'x5', 'x6', 'x7')
 W_CHUNK = 256
 STD_LAG = 2
+CG0 = 2
 OUT_LAG = 3
+TLAG = 1
+TC = 0
 
 
 def tile_onebitlinear_kernel(
@@ -65,6 +68,9 @@ def tile_onebitlinear_kernel(
         nc.vector.memset(vec_rows_bf[:], 0.0)
         eps = const.tile([P, 1], F32, name="eps")
         nc.vector.memset(eps[:], LN_EPS)
+        stats_all = const.tile([P, ROW_TILES, 24], F32, name="stats_all")
+        nc.vector.memset(stats_all[:], float(BANK))
+        used = {}
         ident = const.tile([P, P], F32, name="ident")
         masks.make_identity(nc, ident[:])
 
@@ -92,7 +98,7 @@ def tile_onebitlinear_kernel(
                     nc.sync.dma_start(out=x_tiles[t][:, cols], in_=x_rows[t * P : (t + 1) * P, cols])
             elif what == "p":
                 for q in range(4):
-                    nc.scalar.dma_start(
+                    nc.sync.dma_start(
                         out=w_planes[32 * q : 32 * q + 16, :].bitcast(I32),
                         in_=weight_scales[:, 4 * q : 4 * q + 4, :].bitcast(I32),
                     )
@@ -111,7 +117,7 @@ def tile_onebitlinear_kernel(
         vec_rows = const.tile([P, P], F32, name="vec_rows")
         scale_bias = const.tile([P, 2 * CHANNEL_TILES], F32, name="scale_bias")
 
-        perm = {}
+        perm, nmr, made = {}, {}, {}
         xt, grouped, codes, planes = {}, {}, {}, {}
         h_t, h_banks, stats, mv, rstd, res, fin = {}, {}, {}, {}, {}, {}, {}
         block_of = {t: b for b, tiles in enumerate(BLOCKS) for t in tiles}
@@ -170,7 +176,7 @@ def tile_onebitlinear_kernel(
             per = BANK // n
             if bank == 0:
                 h_t[b] = hpool.tile([P, CHANNEL_TILES, n], F32, name="h_t")
-            acc = psum_mm.tile([P, per, n], F32, name="acc")
+            acc = psum_mm.tile([P, per, n], F32, name="acc", tag="acc")
             for jj in range(per):
                 chans = slice((bank * per + jj) * P, (bank * per + jj + 1) * P)
                 for g in range(PASSES):
@@ -185,6 +191,12 @@ def tile_onebitlinear_kernel(
                     )
             for jj in range(per):
                 j = bank * per + jj
+                if b == len(BLOCKS) - 1 and bank == 3 and jj in ():
+                    nc.vector.tensor_scalar(
+                        out=h_t[b][:, j, :], in0=acc[:, jj, :], scalar1=scale_bias[:, j : j + 1],
+                        scalar2=scale_bias[:, CHANNEL_TILES + j : CHANNEL_TILES + j + 1], op0=ALU.mult, op1=ALU.add,
+                    )
+                    continue
                 nc.scalar.activation(
                     out=h_t[b][:, j, :],
                     in_=acc[:, jj, :],
@@ -198,8 +210,10 @@ def tile_onebitlinear_kernel(
             part = BLOCKS[b].index(t)
             if c == 0:
                 h_banks[t] = []
-            if TAIL and t == ROW_TILES - 1 and c < 2:
+            if t == ROW_TILES - 1 and c < 2:
                 bank = psum_x.tile([P, BANK], F32, name="h_last", tag="xt")
+            elif t == ROW_TILES - 1:
+                bank = psum_mm.tile([P, BANK], F32, name="h_last", tag="acc")
             else:
                 bank = psum_h.tile([P, BANK], F32, name="h_bank")
             for jj in range(4):
@@ -209,17 +223,35 @@ def tile_onebitlinear_kernel(
             h_banks[t].append(bank)
 
         def row_stats(t, c):
-            if c == 0:
-                stats[t] = small.tile([P, BANKS_PER_ROW, 6], F32, name="stats")
-            nc.vector.bn_stats(out=stats[t][:, c, :], in_=h_banks[t][c][:])
+            n_used = used.get(t, 0)
+            bank = h_banks[t][c]
+            if c not in S_STATS.get(t, ()):
+                nc.vector.bn_stats(out=stats_all[:, t, n_used : n_used + 6], in_=bank[:])
+                used[t] = n_used + 6
+                return
+            neg = small.tile([P, 2], F32, name="neg")
+            junk = work.tile([P, BANK], F32, name="junk")
+            nc.scalar.activation(out=junk[:], in_=bank[:], func=ACT.Copy, accum_out=neg[:, 0:1])
+            nc.scalar.activation(out=neg[:, 1:2], in_=neg[:, 0:1], func=ACT.Copy, scale=-1.0 / BANK)
+            junk = work.tile([P, BANK], F32, name="junk")
+            nc.scalar.activation(
+                out=junk[:], in_=bank[:], func=ACT.Square, bias=neg[:, 1:2], scale=1.0,
+                accum_out=stats_all[:, t, n_used + 2 : n_used + 3],
+            )
+            nc.scalar.activation(
+                out=stats_all[:, t, n_used + 1 : n_used + 2], in_=neg[:, 0:1], func=ACT.Copy, scale=1.0 / BANK
+            )
+            used[t] = n_used + 3
 
         def aggregate(t):
             mv[t] = small.tile([P, 2], F32, name="mean_var")
-            nc.vector.bn_aggr(out=mv[t][:], in_=stats[t][:].rearrange("p c s -> p (c s)"))
+            nc.vector.bn_aggr(out=mv[t][:], in_=stats_all[:, t, 0 : used[t]])
 
         def centre_and_gain(t, c):
-            if c == 0:
+            if t not in res:
                 res[t] = work.tile([P, D_OUT], F32, name="res")
+            if c in G_GAIN.get(t, ()):
+                return
             cols = slice(c * BANK, (c + 1) * BANK)
             nc.vector.scalar_tensor_tensor(
                 out=res[t][:, cols], in0=h_banks[t][c][:], scalar=mv[t][:, 0:1], in1=gamma_bc[:, cols],
@@ -232,19 +264,34 @@ def tile_onebitlinear_kernel(
 
         def inverse_std(t):
             nc.vector.reciprocal(rstd[t][:, 1:2], rstd[t][:, 0:1])
+            if t in G_GAIN:
+                nmr[t] = small.tile([P, 1], F32, name="nmr")
+                nc.vector.scalar_tensor_tensor(
+                    out=nmr[t][:], in0=mv[t][:, 0:1], scalar=-1.0, in1=rstd[t][:, 1:2], op0=ALU.mult, op1=ALU.mult
+                )
 
         def scale_rows(t, c):
-            if c == 0:
+            if t not in fin:
                 fin[t] = work.tile([P, D_OUT], F32, name="fin")
             cols = slice(c * BANK, (c + 1) * BANK)
-            nc.scalar.activation(out=fin[t][:, cols], in_=res[t][:, cols], func=ACT.Copy, scale=rstd[t][:, 1:2])
+            if c in G_GAIN.get(t, ()):
+                nc.scalar.activation(
+                    out=res[t][:, cols], in_=h_banks[t][c][:], func=ACT.Identity, scale=rstd[t][:, 1:2], bias=nmr[t][:]
+                )
+                nc.gpsimd.tensor_tensor(out=fin[t][:, cols], in0=res[t][:, cols], in1=gamma_bc[:, cols], op=ALU.mult)
+            else:
+                nc.scalar.activation(out=fin[t][:, cols], in_=res[t][:, cols], func=ACT.Copy, scale=rstd[t][:, 1:2])
             nc.gpsimd.tensor_tensor(out=fin[t][:, cols], in0=fin[t][:, cols], in1=beta_bc[:, cols], op=ALU.add)
-            if c % 2:
-                store(t, fin[t], c - 1, c + 1)
+            made.setdefault(t, set()).add(c)
+            if t == ROW_TILES - 1:
+                store(t, fin[t], c, c + 1)
+            elif c // 2 * 2 in made[t] and c // 2 * 2 + 1 in made[t]:
+                store(t, fin[t], c // 2 * 2, c // 2 * 2 + 2)
 
         def store(t, tile, c0, c1):
             cols = slice(c0 * BANK, c1 * BANK)
-            nc.sync.dma_start(out=out_rows[t * P : (t + 1) * P, cols], in_=tile[:, cols])
+            queue = nc.scalar if t == ROW_TILES - 1 else nc.sync
+            queue.dma_start(out=out_rows[t * P : (t + 1) * P, cols], in_=tile[:, cols])
 
         def finish_on_vector(t, c):
             cols = slice(c * BANK, (c + 1) * BANK)
@@ -255,13 +302,15 @@ def tile_onebitlinear_kernel(
             store(t, res[t], c, c + 1)
 
         later = {}
+        LAST = ROW_TILES - 1
         transpose_x(0)
         nc.scalar.copy(out=vec_rows[:], in_=vec_rows_bf[:])
         scale_x(0)
-        quantise(0)
+        if len(BLOCKS[0]) == 1:
+            quantise(0)
         transpose_x(1)
         scale_x(1)
-        quantise(1)
+        quantise(1 if len(BLOCKS[0]) == 1 else 0)
         vec_cols = psum_h.tile([P, BANK], F32, name="h_bank")
         nc.tensor.transpose(vec_cols[:, 0:P], vec_rows[:], ident[:])
         nc.scalar.copy(out=scale_bias[:], in_=vec_cols[:, 0 : 2 * CHANNEL_TILES])
@@ -272,56 +321,57 @@ def tile_onebitlinear_kernel(
                     permute_x(t)
             for job in later.pop(k, []):
                 job()
-            if TAIL:
-                t = ROW_TILES - 1
-                for c in range(2):
-                    if k == SLOTS.index((t, c)) + 1:
-                        transpose_h(t, c)
-                        row_stats(t, c)
             for t in range(ROW_TILES):
                 if XT_AT.get(t) == k:
                     transpose_x(t)
-            for t in range(ROW_TILES - 1):
+            for t in range(LAST):
                 if HT_AT.get(t) == k:
                     for c in range(4):
                         transpose_h(t, c)
+            for c in range(TC):
+                if k == len(SLOTS) - TC + c:
+                    transpose_h(LAST, c)
             for t in range(ROW_TILES):
                 if XT_AT.get(t) == k:
                     scale_x(t)
-            for t in range(ROW_TILES - 1):
+            for t in range(LAST):
                 if HT_AT.get(t) == k:
                     for c in range(4):
                         row_stats(t, c)
             for t in range(ROW_TILES):
-                if XT_AT.get(t) == k:
-                    quantise(t)
-            for t in range(ROW_TILES - 1):
+                if XT_AT.get(t) == k and t == BLOCKS[block_of[t]][-1]:
+                    quantise(block_of[t])
+            for t in range(LAST):
                 if HT_AT.get(t) == k:
                     aggregate(t)
-                    for c in range(4):
+                    for c in range(CG0):
                         centre_and_gain(t, c)
-                    later.setdefault(k + STD_LAG, []).append(lambda t=t: (std_dev(t), inverse_std(t)))
-                    for c in range(4):
-                        later.setdefault(k + OUT_LAG + c, []).append(lambda t=t, c=c: scale_rows(t, c))
+                    lag = STD_LAG if t < LAST - 1 else 1
+                    later.setdefault(k + lag, []).append(
+                        lambda t=t: (std_dev(t), inverse_std(t), [centre_and_gain(t, c) for c in range(CG0, 4)])
+                    )
+                    first = G_GAIN.get(t, ())
+                    for c in first:
+                        later.setdefault(k + STD_LAG + 0, []).append(lambda t=t, c=c: scale_rows(t, c))
+                    for i, c in enumerate([c for c in range(4) if c not in first]):
+                        later.setdefault(k + (OUT_LAG if t < LAST - 1 else 2) + i, []).append(lambda t=t, c=c: scale_rows(t, c))
+        t = LAST
+        for c in range(TC, 4):
+            transpose_h(t, c)
         for k in sorted(later):
             for job in later[k]:
                 job()
-        t = ROW_TILES - 1
-        if not TAIL:
-            for c in range(4):
-                transpose_h(t, c)
-            for c in range(4):
-                row_stats(t, c)
-        else:
-            for c in range(2, 4):
-                transpose_h(t, c)
-                row_stats(t, c)
+        for c in range(4):
+            row_stats(t, c)
         aggregate(t)
         std_dev(t)
         centre_and_gain(t, 0)
         centre_and_gain(t, 1)
         inverse_std(t)
+        for c in G_GAIN.get(t, ()):
+            scale_rows(t, c)
         for c in range(4):
-            finish_on_vector(t, c)
+            if c not in G_GAIN.get(t, ()):
+                finish_on_vector(t, c)
             if c < 2:
                 centre_and_gain(t, c + 2)

@@ -36,7 +36,7 @@ G_GAIN = {}
 LOADS = ('x0', 'p', 'x1', 'w0', 'w1', 'w2', 'w3', 'w4', 'w5', 'x2', 'w6', 'w7', 'x3', 'gb', 'x4', 'x5', 'x6', 'x7')
 W_CHUNK = 256
 STD_LAG = 2
-CG0 = 2
+CG0 = 4
 OUT_LAG = 3
 TLAG = 1
 TC = 0
@@ -71,17 +71,18 @@ def tile_onebitlinear_kernel(
         stats_all = const.tile([P, ROW_TILES, 24], F32, name="stats_all")
         nc.vector.memset(stats_all[:], float(BANK))
         used = {}
-        ident = const.tile([P, P], F32, name="ident")
-        masks.make_identity(nc, ident[:])
 
         s_cols = const.tile([P, PASSES, PACK], BF16, name="s_cols")
-        nc.scalar.dma_start(out=s_cols[:], in_=in_channel_scale.rearrange("(g p t) -> p g t", p=P, t=PACK))
-        nc.scalar.dma_start(
+        nc.gpsimd.dma_start(out=s_cols[:], in_=in_channel_scale.rearrange("(g p t) -> p g t", p=P, t=PACK))
+        nc.gpsimd.dma_start(
             out=vec_rows_bf[0:CHANNEL_TILES, :], in_=out_channel_scale.rearrange("(j c) -> j c", c=P)
         )
-        nc.scalar.dma_start(
+        nc.gpsimd.dma_start(
             out=vec_rows_bf[CHANNEL_TILES : 2 * CHANNEL_TILES, :], in_=bias.rearrange("(j c) -> j c", c=P)
         )
+
+        ident = const.tile([P, P], F32, name="ident")
+        masks.make_identity(nc, ident[:])
 
         x_tiles = {}
         w_words = const.tile([P, PASSES, D_OUT], U32, name="w_words", align_bytes=64)
@@ -98,7 +99,7 @@ def tile_onebitlinear_kernel(
                     nc.sync.dma_start(out=x_tiles[t][:, cols], in_=x_rows[t * P : (t + 1) * P, cols])
             elif what == "p":
                 for q in range(4):
-                    nc.sync.dma_start(
+                    nc.scalar.dma_start(
                         out=w_planes[32 * q : 32 * q + 16, :].bitcast(I32),
                         in_=weight_scales[:, 4 * q : 4 * q + 4, :].bitcast(I32),
                     )

@@ -72,17 +72,17 @@ def tile_onebitlinear_kernel(
         nc.vector.memset(stats_all[:], float(BANK))
         used = {}
 
+        ident = const.tile([P, P], F32, name="ident")
+        masks.make_identity(nc, ident[:])
+
         s_cols = const.tile([P, PASSES, PACK], BF16, name="s_cols")
-        nc.gpsimd.dma_start(out=s_cols[:], in_=in_channel_scale.rearrange("(g p t) -> p g t", p=P, t=PACK))
+        nc.scalar.dma_start(out=s_cols[:], in_=in_channel_scale.rearrange("(g p t) -> p g t", p=P, t=PACK))
         nc.gpsimd.dma_start(
             out=vec_rows_bf[0:CHANNEL_TILES, :], in_=out_channel_scale.rearrange("(j c) -> j c", c=P)
         )
         nc.gpsimd.dma_start(
             out=vec_rows_bf[CHANNEL_TILES : 2 * CHANNEL_TILES, :], in_=bias.rearrange("(j c) -> j c", c=P)
         )
-
-        ident = const.tile([P, P], F32, name="ident")
-        masks.make_identity(nc, ident[:])
 
         x_tiles = {}
         w_words = const.tile([P, PASSES, D_OUT], U32, name="w_words", align_bytes=64)

@@ -118,7 +118,7 @@ def tile_onebitlinear_kernel(
         vec_rows = const.tile([P, P], F32, name="vec_rows")
         scale_bias = const.tile([P, 2 * CHANNEL_TILES], F32, name="scale_bias")
 
-        perm, nmr, made = {}, {}, {}
+        perm, nmr, made, accs = {}, {}, {}, {}
         xt, grouped, codes, planes = {}, {}, {}, {}
         h_t, h_banks, stats, mv, rstd, res, fin = {}, {}, {}, {}, {}, {}, {}
         block_of = {t: b for b, tiles in enumerate(BLOCKS) for t in tiles}
@@ -190,6 +190,12 @@ def tile_onebitlinear_kernel(
                         start=(g == 0),
                         stop=(g == PASSES - 1),
                     )
+            accs[b, bank] = acc
+
+        def empty(b, bank):
+            n = P * len(BLOCKS[b])
+            per = BANK // n
+            acc = accs[b, bank]
             for jj in range(per):
                 j = bank * per + jj
                 if b == len(BLOCKS) - 1 and bank == 3 and jj in ():
@@ -312,11 +318,13 @@ def tile_onebitlinear_kernel(
         transpose_x(1)
         scale_x(1)
         quantise(1 if len(BLOCKS[0]) == 1 else 0)
-        vec_cols = psum_h.tile([P, BANK], F32, name="h_bank")
-        nc.tensor.transpose(vec_cols[:, 0:P], vec_rows[:], ident[:])
-        nc.scalar.copy(out=scale_bias[:], in_=vec_cols[:, 0 : 2 * CHANNEL_TILES])
         for k, (b, bank) in enumerate(SLOTS):
             linear(b, bank)
+            if k == 0:
+                vec_cols = psum_h.tile([P, BANK], F32, name="h_bank")
+                nc.tensor.transpose(vec_cols[:, 0:P], vec_rows[:], ident[:])
+                nc.scalar.copy(out=scale_bias[:], in_=vec_cols[:, 0 : 2 * CHANNEL_TILES])
+            empty(b, bank)
             for t in range(PERM_FROM, ROW_TILES):
                 if XT_AT[t] - PERM_LEAD == k:
                     permute_x(t)
@@ -355,7 +363,7 @@ def tile_onebitlinear_kernel(
                     for c in first:
                         later.setdefault(k + STD_LAG + 0, []).append(lambda t=t, c=c: scale_rows(t, c))
                     for i, c in enumerate([c for c in range(4) if c not in first]):
-                        later.setdefault(k + (OUT_LAG if t < LAST - 1 else 2) + i, []).append(lambda t=t, c=c: scale_rows(t, c))
+                        later.setdefault(k + (OUT_LAG if t < LAST - 1 else 3) + i, []).append(lambda t=t, c=c: scale_rows(t, c))
         t = LAST
         for c in range(TC, 4):
             transpose_h(t, c)

@@ -26,7 +26,7 @@ LN_EPS = 1e-5
 FLOPS = 2 * ROWS * D_IN * D_OUT
 
 BLOCKS = tuple((t,) for t in range(ROW_TILES))
-SLOTS = [(0, 0), (1, 0), (0, 1), (1, 1), (0, 2), (0, 3), (1, 2), (1, 3)] + [(t, c) for t in range(2, 8) for c in range(4)]
+SLOTS = [(0, 0), (1, 0), (0, 1),(1,1), (0, 2), (0, 3), (1, 2), (1, 3)] + [(t, c) for t in range(2, 8) for c in range(4)]
 HT_AT = {t: SLOTS.index((t, 3)) + min(t, 1) for t in range(7)}
 XT_AT = {t: SLOTS.index((t - 1, 0) if t > 2 else (0, 2)) for t in range(2, 8)}
 PERM_FROM = 3
@@ -37,7 +37,8 @@ LOADS = ('x0', 'p', 'x1', 'w0', 'w1', 'w2', 'w3', 'w4', 'w5', 'x2', 'w6', 'w7', 
 W_CHUNK = 256
 STD_LAG = 2
 CG0 = 4
-OUT_LAG = 3
+OUTS = (3, 4, 5, 6)
+OUT6 = (3, 4, 5, 6)
 TLAG = 1
 TC = 0
 
@@ -84,6 +85,7 @@ def tile_onebitlinear_kernel(
             out=vec_rows_bf[CHANNEL_TILES : 2 * CHANNEL_TILES, :], in_=bias.rearrange("(j c) -> j c", c=P)
         )
 
+        LAST = ROW_TILES - 1
         x_tiles = {}
         w_words = const.tile([P, PASSES, D_OUT], U32, name="w_words", align_bytes=64)
         w_bytes = weight_words.rearrange("g p n t -> p g (n t)")
@@ -292,6 +294,8 @@ def tile_onebitlinear_kernel(
             made.setdefault(t, set()).add(c)
             if t == ROW_TILES - 1:
                 store(t, fin[t], c, c + 1)
+            elif t == LAST - 1 and (3,):
+                store(t, fin[t], c, c + 1)
             elif c // 2 * 2 in made[t] and c // 2 * 2 + 1 in made[t]:
                 store(t, fin[t], c // 2 * 2, c // 2 * 2 + 2)
 
@@ -309,7 +313,6 @@ def tile_onebitlinear_kernel(
             store(t, res[t], c, c + 1)
 
         later = {}
-        LAST = ROW_TILES - 1
         transpose_x(0)
         nc.scalar.copy(out=vec_rows[:], in_=vec_rows_bf[:])
         scale_x(0)
@@ -325,11 +328,16 @@ def tile_onebitlinear_kernel(
                 nc.tensor.transpose(vec_cols[:, 0:P], vec_rows[:], ident[:])
                 nc.scalar.copy(out=scale_bias[:], in_=vec_cols[:, 0 : 2 * CHANNEL_TILES])
             empty(b, bank)
-            for t in range(PERM_FROM, ROW_TILES):
-                if XT_AT[t] - PERM_LEAD == k:
-                    permute_x(t)
+            if 1:
+                for t in range(PERM_FROM, ROW_TILES):
+                    if XT_AT[t] - PERM_LEAD == k:
+                        permute_x(t)
             for job in later.pop(k, []):
                 job()
+            if not 1:
+                for t in range(PERM_FROM, ROW_TILES):
+                    if XT_AT[t] - PERM_LEAD == k:
+                        permute_x(t)
             for t in range(ROW_TILES):
                 if XT_AT.get(t) == k:
                     transpose_x(t)
@@ -362,8 +370,9 @@ def tile_onebitlinear_kernel(
                     first = G_GAIN.get(t, ())
                     for c in first:
                         later.setdefault(k + STD_LAG + 0, []).append(lambda t=t, c=c: scale_rows(t, c))
-                    for i, c in enumerate([c for c in range(4) if c not in first]):
-                        later.setdefault(k + (OUT_LAG if t < LAST - 1 else 3) + i, []).append(lambda t=t, c=c: scale_rows(t, c))
+                    for i, c in enumerate([c for c in range(4) if c not in first and not (t == LAST - 1 and c in (3,))]):
+                        later.setdefault(k + (OUTS if t < LAST - 1 else OUT6)[i], []).append(lambda t=t, c=c: scale_rows(t, c))
+        v6 = (3,)
         t = LAST
         for c in range(TC, 4):
             transpose_h(t, c)
@@ -372,15 +381,20 @@ def tile_onebitlinear_kernel(
                 job()
         for c in range(4):
             row_stats(t, c)
+        for c in v6:
+            cols = slice(c * BANK, (c + 1) * BANK)
+            nc.vector.scalar_tensor_tensor(
+                out=res[LAST - 1][:, cols], in0=res[LAST - 1][:, cols], scalar=rstd[LAST - 1][:, 1:2], in1=beta_bc[:, cols],
+                op0=ALU.mult, op1=ALU.add,
+            )
+            nc.sync.dma_start(out=out_rows[(LAST - 1) * P : LAST * P, cols], in_=res[LAST - 1][:, cols])
         aggregate(t)
         std_dev(t)
-        centre_and_gain(t, 0)
-        centre_and_gain(t, 1)
-        inverse_std(t)
-        for c in G_GAIN.get(t, ()):
-            scale_rows(t, c)
-        for c in range(4):
-            if c not in G_GAIN.get(t, ()):
-                finish_on_vector(t, c)
-            if c < 2:
-                centre_and_gain(t, c + 2)
+        ordr = '01r23ABCD'
+        for ch in ordr:
+            if ch == "r":
+                inverse_std(t)
+            elif ch in "0123":
+                centre_and_gain(t, int(ch))
+            else:
+                finish_on_vector(t, "ABCD".index(ch))

from contextlib import ExitStack

import concourse.masks as masks
import concourse.mybir as mybir

F32 = mybir.dt.float32
BF16 = mybir.dt.bfloat16
I32 = mybir.dt.int32
U32 = mybir.dt.uint32
U8 = mybir.dt.uint8
FP8X4 = mybir.dt.float8_e4m3fn_x4
ALU = mybir.AluOpType
ACT = mybir.ActivationFunctionType

P = 128
PACK = 4
ROWS = 1024
D_IN = 2048
D_OUT = 2048
PASSES = D_IN // (P * PACK)
ROW_TILES = ROWS // P
CHANNEL_TILES = D_OUT // P
BANK = 512
BANKS_PER_ROW = D_OUT // BANK
LN_EPS = 1e-5
FLOPS = 2 * ROWS * D_IN * D_OUT

BLOCKS = tuple((t,) for t in range(ROW_TILES))
SLOTS = [(0, 0), (1, 0), (0, 1),(1,1), (0, 2), (0, 3), (1, 2), (1, 3)] + [(t, c) for t in range(2, 8) for c in range(4)]
HT_AT = {t: SLOTS.index((t, 3)) + min(t, 1) for t in range(7)}
XT_AT = {t: SLOTS.index((t - 1, 0) if t > 2 else (0, 2)) for t in range(2, 8)}
PERM_FROM = 3
PERM_LEAD = 2
S_STATS = {}
G_GAIN = {}
LOADS = ('x0', 'p', 'x1', 'w0', 'w1', 'w2', 'w3', 'w4', 'w5', 'x2', 'w6', 'w7', 'x3', 'gb', 'x4', 'x5', 'x6', 'x7')
W_CHUNK = 256
STD_LAG = 2
CG0 = 4
OUTS = (3, 4, 5, 6)
OUT6 = (3, 4, 5, 6)
TLAG = 1
TC = 0


def tile_onebitlinear_kernel(
    tc, x, weight_words, weight_scales, in_channel_scale, out_channel_scale, bias, ln_gamma, ln_beta, out
):
    nc = tc.nc
    x_rows = x.flatten_outer_dims()
    out_rows = out.flatten_outer_dims()

    with ExitStack() as ctx:
        const = ctx.enter_context(tc.tile_pool(name="const", bufs=1))
        xin = ctx.enter_context(tc.tile_pool(name="xin", bufs=ROW_TILES))
        xprep = ctx.enter_context(tc.tile_pool(name="xprep", bufs=2))
        xperm = ctx.enter_context(tc.tile_pool(name="xperm", bufs=2))
        hpool = ctx.enter_context(tc.tile_pool(name="hpool", bufs=3))
        work = ctx.enter_context(tc.tile_pool(name="work", bufs=3))
        small = ctx.enter_context(tc.tile_pool(name="small", bufs=3))
        psum_mm = ctx.enter_context(tc.psum_pool(name="psum_mm", bufs=2))
        psum_x = ctx.enter_context(tc.psum_pool(name="psum_x", bufs=2))
        psum_h = ctx.enter_context(tc.psum_pool(name="psum_h", bufs=4))
        ctx.enter_context(tc.manual_schedule())

        w_planes = const.tile([P, D_OUT], U8, name="w_planes", align_bytes=64)
        nc.vector.memset(w_planes[:].bitcast(I32), 0)
        vec_rows_bf = const.tile([P, P], BF16, name="vec_rows_bf")
        nc.vector.memset(vec_rows_bf[:], 0.0)
        eps = const.tile([P, 1], F32, name="eps")
        nc.vector.memset(eps[:], LN_EPS)
        stats_all = const.tile([P, ROW_TILES, 24], F32, name="stats_all")
        nc.vector.memset(stats_all[:], float(BANK))
        used = {}

        ident = const.tile([P, P], F32, name="ident")
        masks.make_identity(nc, ident[:])

        s_cols = const.tile([P, PASSES, PACK], BF16, name="s_cols")
        nc.scalar.dma_start(out=s_cols[:], in_=in_channel_scale.rearrange("(g p t) -> p g t", p=P, t=PACK))
        nc.gpsimd.dma_start(
            out=vec_rows_bf[0:CHANNEL_TILES, :], in_=out_channel_scale.rearrange("(j c) -> j c", c=P)
        )
        nc.gpsimd.dma_start(
            out=vec_rows_bf[CHANNEL_TILES : 2 * CHANNEL_TILES, :], in_=bias.rearrange("(j c) -> j c", c=P)
        )

        LAST = ROW_TILES - 1
        x_tiles = {}
        w_words = const.tile([P, PASSES, D_OUT], U32, name="w_words", align_bytes=64)
        w_bytes = weight_words.rearrange("g p n t -> p g (n t)")
        gamma_bc = const.tile([P, D_OUT], BF16, name="gamma_bc")
        beta_bc = const.tile([P, D_OUT], BF16, name="beta_bc")
        for what in LOADS:
            if what[0] == "x":
                t = int(what[1:])
                x_tiles[t] = xin.tile([P, D_IN], BF16, name="x_sb")
                halves = 2 if t == 0 else 1
                for i in range(halves):
                    cols = slice(i * D_IN // halves, (i + 1) * D_IN // halves)
                    nc.sync.dma_start(out=x_tiles[t][:, cols], in_=x_rows[t * P : (t + 1) * P, cols])
            elif what == "p":
                for q in range(4):
                    nc.scalar.dma_start(
                        out=w_planes[32 * q : 32 * q + 16, :].bitcast(I32),
                        in_=weight_scales[:, 4 * q : 4 * q + 4, :].bitcast(I32),
                    )
            elif what[0] == "w":
                c = int(what[1:])
                nc.sync.dma_start(
                    out=w_words[:, :, c * W_CHUNK : (c + 1) * W_CHUNK].bitcast(I32),
                    in_=w_bytes[:, :, c * W_CHUNK * PACK : (c + 1) * W_CHUNK * PACK].bitcast(I32),
                )
            else:
                nc.sync.dma_start(out=gamma_bc[:], in_=ln_gamma.partition_broadcast(P))
                nc.sync.dma_start(out=beta_bc[:], in_=ln_beta.partition_broadcast(P))

        first_table = const.tile([P, 1], F32, name="first_table")
        nc.scalar.activation(out=first_table[:], in_=eps[:], func=ACT.Sqrt)
        vec_rows = const.tile([P, P], F32, name="vec_rows")
        scale_bias = const.tile([P, 2 * CHANNEL_TILES], F32, name="scale_bias")

        perm, nmr, made, accs = {}, {}, {}, {}
        xt, grouped, codes, planes = {}, {}, {}, {}
        h_t, h_banks, stats, mv, rstd, res, fin = {}, {}, {}, {}, {}, {}, {}
        block_of = {t: b for b, tiles in enumerate(BLOCKS) for t in tiles}

        def permute_x(t):
            perm[t] = xperm.tile([P, PASSES, 2, P], F32, name="x_perm", align_bytes=64)
            nc.scalar.copy(
                out=perm[t][:], in_=x_tiles[t][:].bitcast(F32).rearrange("p (g w u) -> p g u w", g=PASSES, u=2)
            )

        def transpose_x(t):
            words = x_tiles[t][:].bitcast(F32)
            xt[t] = []
            for pair in range(PASSES // 2):
                bank = psum_x.tile([P, 2, 2, P], F32, name="xt", tag="xt")
                for gg in range(2):
                    g = 2 * pair + gg
                    for u in range(2):
                        if t in perm:
                            some = perm[t][:, g, u, :]
                        else:
                            some = words[:, 256 * g + u : 256 * (g + 1) : 2]
                        nc.tensor.transpose(bank[:, gg, u, :], some, ident[:])
                xt[t].append(bank)

        def scale_x(t):
            b = block_of[t]
            n = P * len(BLOCKS[b])
            part = BLOCKS[b].index(t)
            if part == 0:
                grouped[b] = xprep.tile([P, PASSES, n, PACK], BF16, name="grouped", align_bytes=64)
            for g in range(PASSES):
                x_t = xt[t][g // 2][:].bitcast(BF16).rearrange("p g u (r e) -> p g r u e", e=2)
                nc.vector.tensor_tensor(
                    out=grouped[b][:, g, part * P : (part + 1) * P, :].rearrange("p r (u e) -> p r u e", e=2),
                    in0=x_t[:, g % 2],
                    in1=s_cols[:, g, :].rearrange("p (u e) -> p u e", e=2).unsqueeze(1).to_broadcast([P, P, 2, 2]),
                    op=ALU.mult,
                )

        def quantise(b):
            n = P * len(BLOCKS[b])
            codes[b] = xprep.tile([P, PASSES, n], U32, name="x_codes", align_bytes=64)
            planes[b] = xprep.tile([P, PASSES, n], U8, name="x_planes", align_bytes=64)
            step = min(PASSES, 2048 // (n * PACK))
            for g0 in range(0, PASSES, step):
                some = slice(g0, g0 + step)
                nc.vector.quantize_mx(
                    out=codes[b][:, some, :].rearrange("p g r -> p (g r)").bitcast(FP8X4),
                    scales=planes[b][:, some, :].rearrange("p g r -> p (g r)"),
                    in_=grouped[b][:, some, :, :].rearrange("p g r t -> p (g r t)"),
                )

        def linear(b, bank):
            n = P * len(BLOCKS[b])
            per = BANK // n
            if bank == 0:
                h_t[b] = hpool.tile([P, CHANNEL_TILES, n], F32, name="h_t")
            acc = psum_mm.tile([P, per, n], F32, name="acc", tag="acc")
            for jj in range(per):
                chans = slice((bank * per + jj) * P, (bank * per + jj + 1) * P)
                for g in range(PASSES):
                    nc.tensor.matmul_mx(
                        out=acc[:, jj, :],
                        lhsT=w_words[:, g, chans].bitcast(FP8X4),
                        lhsT_scale=w_planes[4 * g : P, chans],
                        rhs=codes[b][:, g, :].bitcast(FP8X4),
                        rhs_scale=planes[b][:, g, :],
                        start=(g == 0),
                        stop=(g == PASSES - 1),
                    )
            accs[b, bank] = acc

        def empty(b, bank):
            n = P * len(BLOCKS[b])
            per = BANK // n
            acc = accs[b, bank]
            for jj in range(per):
                j = bank * per + jj
                if b == len(BLOCKS) - 1 and bank == 3 and jj in ():
                    nc.vector.tensor_scalar(
                        out=h_t[b][:, j, :], in0=acc[:, jj, :], scalar1=scale_bias[:, j : j + 1],
                        scalar2=scale_bias[:, CHANNEL_TILES + j : CHANNEL_TILES + j + 1], op0=ALU.mult, op1=ALU.add,
                    )
                    continue
                nc.scalar.activation(
                    out=h_t[b][:, j, :],
                    in_=acc[:, jj, :],
                    func=ACT.Identity,
                    scale=scale_bias[:, j : j + 1],
                    bias=scale_bias[:, CHANNEL_TILES + j : CHANNEL_TILES + j + 1],
                )

        def transpose_h(t, c):
            b = block_of[t]
            part = BLOCKS[b].index(t)
            if c == 0:
                h_banks[t] = []
            if t == ROW_TILES - 1 and c < 2:
                bank = psum_x.tile([P, BANK], F32, name="h_last", tag="xt")
            elif t == ROW_TILES - 1:
                bank = psum_mm.tile([P, BANK], F32, name="h_last", tag="acc")
            else:
                bank = psum_h.tile([P, BANK], F32, name="h_bank")
            for jj in range(4):
                nc.tensor.transpose(
                    bank[:, jj * P : (jj + 1) * P], h_t[b][:, 4 * c + jj, part * P : (part + 1) * P], ident[:]
                )
            h_banks[t].append(bank)

        def row_stats(t, c):
            n_used = used.get(t, 0)
            bank = h_banks[t][c]
            if c not in S_STATS.get(t, ()):
                nc.vector.bn_stats(out=stats_all[:, t, n_used : n_used + 6], in_=bank[:])
                used[t] = n_used + 6
                return
            neg = small.tile([P, 2], F32, name="neg")
            junk = work.tile([P, BANK], F32, name="junk")
            nc.scalar.activation(out=junk[:], in_=bank[:], func=ACT.Copy, accum_out=neg[:, 0:1])
            nc.scalar.activation(out=neg[:, 1:2], in_=neg[:, 0:1], func=ACT.Copy, scale=-1.0 / BANK)
            junk = work.tile([P, BANK], F32, name="junk")
            nc.scalar.activation(
                out=junk[:], in_=bank[:], func=ACT.Square, bias=neg[:, 1:2], scale=1.0,
                accum_out=stats_all[:, t, n_used + 2 : n_used + 3],
            )
            nc.scalar.activation(
                out=stats_all[:, t, n_used + 1 : n_used + 2], in_=neg[:, 0:1], func=ACT.Copy, scale=1.0 / BANK
            )
            used[t] = n_used + 3

        def aggregate(t):
            mv[t] = small.tile([P, 2], F32, name="mean_var")
            nc.vector.bn_aggr(out=mv[t][:], in_=stats_all[:, t, 0 : used[t]])

        def centre_and_gain(t, c):
            if t not in res:
                res[t] = work.tile([P, D_OUT], F32, name="res")
            if c in G_GAIN.get(t, ()):
                return
            cols = slice(c * BANK, (c + 1) * BANK)
            nc.vector.scalar_tensor_tensor(
                out=res[t][:, cols], in0=h_banks[t][c][:], scalar=mv[t][:, 0:1], in1=gamma_bc[:, cols],
                op0=ALU.subtract, op1=ALU.mult,
            )

        def std_dev(t):
            rstd[t] = small.tile([P, 2], F32, name="rstd")
            nc.scalar.activation(out=rstd[t][:, 0:1], in_=mv[t][:, 1:2], func=ACT.Sqrt, bias=eps[:], scale=1.0)

        def inverse_std(t):
            nc.vector.reciprocal(rstd[t][:, 1:2], rstd[t][:, 0:1])
            if t in G_GAIN:
                nmr[t] = small.tile([P, 1], F32, name="nmr")
                nc.vector.scalar_tensor_tensor(
                    out=nmr[t][:], in0=mv[t][:, 0:1], scalar=-1.0, in1=rstd[t][:, 1:2], op0=ALU.mult, op1=ALU.mult
                )

        def scale_rows(t, c):
            if t not in fin:
                fin[t] = work.tile([P, D_OUT], F32, name="fin")
            cols = slice(c * BANK, (c + 1) * BANK)
            if c in G_GAIN.get(t, ()):
                nc.scalar.activation(
                    out=res[t][:, cols], in_=h_banks[t][c][:], func=ACT.Identity, scale=rstd[t][:, 1:2], bias=nmr[t][:]
                )
                nc.gpsimd.tensor_tensor(out=fin[t][:, cols], in0=res[t][:, cols], in1=gamma_bc[:, cols], op=ALU.mult)
            else:
                nc.scalar.activation(out=fin[t][:, cols], in_=res[t][:, cols], func=ACT.Copy, scale=rstd[t][:, 1:2])
            nc.gpsimd.tensor_tensor(out=fin[t][:, cols], in0=fin[t][:, cols], in1=beta_bc[:, cols], op=ALU.add)
            made.setdefault(t, set()).add(c)
            if t == ROW_TILES - 1:
                store(t, fin[t], c, c + 1)
            elif t == LAST - 1 and (3,):
                store(t, fin[t], c, c + 1)
            elif c // 2 * 2 in made[t] and c // 2 * 2 + 1 in made[t]:
                store(t, fin[t], c // 2 * 2, c // 2 * 2 + 2)

        def store(t, tile, c0, c1):
            cols = slice(c0 * BANK, c1 * BANK)
            queue = nc.scalar if t == ROW_TILES - 1 else nc.sync
            queue.dma_start(out=out_rows[t * P : (t + 1) * P, cols], in_=tile[:, cols])

        def finish_on_vector(t, c):
            cols = slice(c * BANK, (c + 1) * BANK)
            nc.vector.scalar_tensor_tensor(
                out=res[t][:, cols], in0=res[t][:, cols], scalar=rstd[t][:, 1:2], in1=beta_bc[:, cols],
                op0=ALU.mult, op1=ALU.add,
            )
            store(t, res[t], c, c + 1)

        later = {}
        transpose_x(0)
        nc.scalar.copy(out=vec_rows[:], in_=vec_rows_bf[:])
        scale_x(0)
        if len(BLOCKS[0]) == 1:
            quantise(0)
        transpose_x(1)
        scale_x(1)
        quantise(1 if len(BLOCKS[0]) == 1 else 0)
        for k, (b, bank) in enumerate(SLOTS):
            linear(b, bank)
            if k == 0:
                vec_cols = psum_h.tile([P, BANK], F32, name="h_bank")
                nc.tensor.transpose(vec_cols[:, 0:P], vec_rows[:], ident[:])
                nc.scalar.copy(out=scale_bias[:], in_=vec_cols[:, 0 : 2 * CHANNEL_TILES])
            empty(b, bank)
            if 1:
                for t in range(PERM_FROM, ROW_TILES):
                    if XT_AT[t] - PERM_LEAD == k:
                        permute_x(t)
            for job in later.pop(k, []):
                job()
            if not 1:
                for t in range(PERM_FROM, ROW_TILES):
                    if XT_AT[t] - PERM_LEAD == k:
                        permute_x(t)
            for t in range(ROW_TILES):
                if XT_AT.get(t) == k:
                    transpose_x(t)
            for t in range(LAST):
                if HT_AT.get(t) == k:
                    for c in range(4):
                        transpose_h(t, c)
            for c in range(TC):
                if k == len(SLOTS) - TC + c:
                    transpose_h(LAST, c)
            for t in range(ROW_TILES):
                if XT_AT.get(t) == k:
                    scale_x(t)
            for t in range(LAST):
                if HT_AT.get(t) == k:
                    for c in range(4):
                        row_stats(t, c)
            for t in range(ROW_TILES):
                if XT_AT.get(t) == k and t == BLOCKS[block_of[t]][-1]:
                    quantise(block_of[t])
            for t in range(LAST):
                if HT_AT.get(t) == k:
                    aggregate(t)
                    for c in range(CG0):
                        centre_and_gain(t, c)
                    lag = STD_LAG if t < LAST - 1 else 1
                    later.setdefault(k + lag, []).append(
                        lambda t=t: (std_dev(t), inverse_std(t), [centre_and_gain(t, c) for c in range(CG0, 4)])
                    )
                    first = G_GAIN.get(t, ())
                    for c in first:
                        later.setdefault(k + STD_LAG + 0, []).append(lambda t=t, c=c: scale_rows(t, c))
                    for i, c in enumerate([c for c in range(4) if c not in first and not (t == LAST - 1 and c in (3,))]):
                        later.setdefault(k + (OUTS if t < LAST - 1 else OUT6)[i], []).append(lambda t=t, c=c: scale_rows(t, c))
        v6 = (3,)
        t = LAST
        for c in range(TC, 4):
            transpose_h(t, c)
        for k in sorted(later):
            for job in later[k]:
                job()
        for c in range(4):
            row_stats(t, c)
        for c in v6:
            cols = slice(c * BANK, (c + 1) * BANK)
            nc.vector.scalar_tensor_tensor(
                out=res[LAST - 1][:, cols], in0=res[LAST - 1][:, cols], scalar=rstd[LAST - 1][:, 1:2], in1=beta_bc[:, cols],
                op0=ALU.mult, op1=ALU.add,
            )
            nc.sync.dma_start(out=out_rows[(LAST - 1) * P : LAST * P, cols], in_=res[LAST - 1][:, cols])
        aggregate(t)
        std_dev(t)
        ordr = '01r23ABCD'
        for ch in ordr:
            if ch == "r":
                inverse_std(t)
            elif ch in "0123":
                centre_and_gain(t, int(ch))
            else:
                finish_on_vector(t, "ABCD".index(ch))
